import numpy as np
import ml_dtypes


def mxq(x, axis, fmt="e4m3"):
    dtype, down = {"e4m3": (ml_dtypes.float8_e4m3fn, 7), "e5m2": (ml_dtypes.float8_e5m2, 14)}[fmt]
    v = np.moveaxis(np.asarray(x, np.float32).astype(ml_dtypes.bfloat16).astype(np.float64), axis, -1)
    blocks = v.reshape(v.shape[:-1] + (-1, 32))
    amax = np.abs(blocks).max(-1, keepdims=True)
    byte = np.maximum(np.where(amax > 0, np.frexp(amax)[1] - 1 + 127, 0) - down, 1)
    scale = np.exp2(byte - 127.0)
    codes = (blocks / scale).astype(np.float32).astype(dtype).astype(np.float64)
    return np.moveaxis((codes * scale).reshape(v.shape), -1, axis)


WIDE = False


def mx_kscale(k):
    if not WIDE:
        return np.ones(k)
    levels = np.array([10, -10, 5, -5, 0])
    if k % 512:
        return np.exp2(np.random.permutation(np.resize(levels, k // 32))).repeat(32)
    a = np.empty((k // 512, 16))
    for p in range(k // 512):
        a[p, :8] = np.random.permutation(np.resize(levels, 8))
        for g in range(8):
            far = levels[np.abs(levels - a[p, g]) >= 10]
            a[p, g + 8] = far[np.random.randint(len(far))]
    return np.exp2(a.ravel()).repeat(32)


BF16 = ml_dtypes.bfloat16


def bf(x):
    return np.asarray(x, np.float32).astype(BF16)


def f64(x):
    return np.asarray(x).astype(np.float64)


N, C, HH, WW = 4, 1024, 16, 16
S = HH * WW
EPS = 1e-5


def setup_inputs():
    s = mx_kscale(C)
    contrast = np.exp2(np.random.uniform(-8.0, 1.0, (N, 1, HH, WW)))
    shift = 0.5 * np.random.standard_normal((N, 1, HH, WW))
    w = 1.0 / np.sqrt(C)
    return {"x": bf(contrast * (np.random.standard_normal((N, C, HH, WW)) + shift)),
            "ln_gamma": bf((1.0 + 0.1 * np.random.standard_normal(C)) * s),
            "ln_beta": bf(0.3 * np.random.standard_normal(C) * s),
            "Wq": bf(np.random.standard_normal((C, C)) * w / s[None, :]),
            "bq": bf(0.3 * np.random.standard_normal(C)),
            "Wk": bf(np.random.standard_normal((C, C)) * w / s[None, :]),
            "bk": bf(0.3 * np.random.standard_normal(C)),
            "Wv": bf(np.random.standard_normal((C, C)) * w / s[None, :]),
            "bv": bf(0.3 * np.random.standard_normal(C))}


def reference(x, ln_gamma, ln_beta, Wq, bq, Wk, bk, Wv, bv):
    xs = f64(x).reshape(N, C, S).swapaxes(1, 2)
    mu = xs.mean(-1, keepdims=True)
    var = xs.var(-1, keepdims=True)
    x_ln = (xs - mu) / np.sqrt(var + EPS) * f64(ln_gamma) + f64(ln_beta)
    xq = mxq(x_ln, 2, "e4m3")
    q = (xq @ mxq(f64(Wq), 1, "e4m3").T) + f64(bq)
    k = (xq @ mxq(f64(Wk), 1, "e4m3").T) + f64(bk)
    v = (xq @ mxq(f64(Wv), 1, "e4m3").T) + f64(bv)
    return q, k, v

@@ -1,0 +1,268 @@
+from contextlib import ExitStack
+
+import concourse.mybir as mybir
+from concourse.masks import make_identity
+
+BF16 = mybir.dt.bfloat16
+F32 = mybir.dt.float32
+U32 = mybir.dt.uint32
+U8 = mybir.dt.uint8
+FP8X4 = mybir.dt.float8_e4m3fn_x4
+ACT = mybir.ActivationFunctionType
+ALU = mybir.AluOpType
+
+P = 128
+IMAGES = 4
+CHANNELS = 1024
+IMAGE_PIXELS = 256
+OUTPUTS = 1024
+PROJECTIONS = 3
+EPS = 1e-5
+
+PACK = 4
+PASSES = CHANNELS // (P * PACK)
+CHUNKS = CHANNELS // P
+STRIPS = IMAGE_PIXELS // P
+BANK = 512
+HALVES = OUTPUTS // BANK
+UNIT_BANKS = 4
+STATS_WIDTH = 512
+STATS_CALLS = CHANNELS // STATS_WIDTH
+STATS_DIM = 6
+
+FLOPS = 2 * IMAGES * IMAGE_PIXELS * CHANNELS * PROJECTIONS * OUTPUTS
+
+
+def tile_selfscaleddotproductattention2d_pa_kernel(
+    tc, x, ln_gamma, ln_beta, Wq, bq, Wk, bk, Wv, bv, out_0, out_1, out_2
+):
+    nc = tc.nc
+    weights = (Wq, Wk, Wv)
+    biases = (bq, bk, bv)
+    outs = (out_0, out_1, out_2)
+
+    with ExitStack() as ctx:
+        keep = ctx.enter_context(tc.tile_pool(name="keep", bufs=1))
+        per_weight = ctx.enter_context(tc.tile_pool(name="per_weight", bufs=PROJECTIONS))
+        work = ctx.enter_context(tc.tile_pool(name="work", bufs=2))
+        psum_unit = ctx.enter_context(tc.psum_pool(name="psum_unit", bufs=UNIT_BANKS))
+        psum_acc = ctx.enter_context(tc.psum_pool(name="psum_acc", bufs=4))
+        ctx.enter_context(tc.manual_schedule())
+
+        x_sb = keep.tile([P, IMAGES, PASSES, PACK * IMAGE_PIXELS], BF16)
+        for n in range(IMAGES):
+            nc.sync.dma_start(
+                out=x_sb[:, n], in_=x[n].rearrange("(g p t) h w -> p g (t h w)", p=P, t=PACK)
+            )
+
+        gamma_bf = keep.tile([P, CHUNKS], BF16)
+        beta_bf = keep.tile([P, CHUNKS], BF16)
+        for vector_sb, vector in ((gamma_bf, ln_gamma), (beta_bf, ln_beta)):
+            nc.scalar.dma_start(
+                out=vector_sb[:].rearrange("p (g t) -> p g t", t=PACK),
+                in_=vector.rearrange("(g p t) -> p g t", p=P, t=PACK),
+            )
+
+        w_sbs = []
+        bias_sb = keep.tile([P, PROJECTIONS, OUTPUTS], BF16)
+        for i in range(PROJECTIONS):
+            w_sb = per_weight.tile([P, OUTPUTS // P, CHANNELS], BF16, name="w_sb")
+            rows = weights[i].rearrange("(r p) k -> p r k", p=P)
+            for oc in range(HALVES):
+                r_range = slice(oc * (BANK // P), (oc + 1) * (BANK // P))
+                nc.sync.dma_start(out=w_sb[:, r_range, :], in_=rows[:, r_range, :])
+            nc.sync.dma_start(out=bias_sb[:, i, :], in_=biases[i].partition_broadcast(P))
+            w_sbs.append(w_sb)
+
+        ident_bf = keep.tile([P, P], BF16)
+        make_identity(nc, ident_bf[:])
+        ident_f = keep.tile([P, P], F32)
+        make_identity(nc, ident_f[:])
+        minus_half = keep.tile([P, STRIPS], F32)
+        nc.gpsimd.memset(minus_half[:], -0.5)
+        gamma = keep.tile([P, CHUNKS], F32)
+        beta = keep.tile([P, CHUNKS], F32)
+        nc.gpsimd.tensor_copy(out=gamma[:], in_=gamma_bf[:])
+        nc.gpsimd.tensor_copy(out=beta[:], in_=beta_bf[:])
+
+        x_pix = keep.tile([P, IMAGES * STRIPS, CHANNELS], BF16)
+        mean_var = keep.tile([P, IMAGES * STRIPS, 2], F32)
+        var_eps = keep.tile([P, IMAGES * STRIPS], F32)
+        rstd = keep.tile([P, IMAGES * STRIPS], F32)
+        minus_mean = keep.tile([P, IMAGES * STRIPS], F32)
+        x_codes = keep.tile([P, IMAGES, PASSES, IMAGE_PIXELS], U32, align_bytes=64)
+        x_scales = keep.tile([P, IMAGES, PASSES, IMAGE_PIXELS], U8, align_bytes=64)
+        w_codes = []
+        w_scales = []
+        for i in range(PROJECTIONS):
+            w_codes.append(per_weight.tile([P, HALVES, PASSES, BANK], U32, align_bytes=64, name="w_codes"))
+            w_scales.append(per_weight.tile([P, HALVES, PASSES, BANK], U8, align_bytes=64, name="w_scales"))
+        normed = []
+
+        def normalise_image(n):
+            strips = slice(n * STRIPS, (n + 1) * STRIPS)
+            for h in range(STRIPS):
+                x_t = psum_unit.tile([P, CHANNELS], BF16, tag="unit", name="x_t")
+                for m in range(CHUNKS):
+                    g, t = divmod(m, PACK)
+                    first = t * IMAGE_PIXELS + h * P
+                    nc.tensor.transpose(
+                        out=x_t[:, m * P : (m + 1) * P],
+                        in_=x_sb[:, n, g, first : first + P],
+                        identity=ident_bf[:],
+                    )
+                nc.scalar.copy(out=x_pix[:, n * STRIPS + h, :], in_=x_t[:])
+            for h in range(STRIPS):
+                b = n * STRIPS + h
+                stats = work.tile([P, STATS_CALLS, STATS_DIM], F32)
+                for s in range(STATS_CALLS):
+                    nc.vector.bn_stats(
+                        out=stats[:, s, :], in_=x_pix[:, b, s * STATS_WIDTH : (s + 1) * STATS_WIDTH]
+                    )
+                nc.vector.bn_aggr(out=mean_var[:, b, :], in_=stats[:].rearrange("p s d -> p (s d)"))
+            nc.gpsimd.tensor_scalar(
+                out=var_eps[:, strips], in0=mean_var[:, strips, 1], scalar1=EPS, scalar2=1.0,
+                op0=ALU.add, op1=ALU.mult,
+            )
+            nc.gpsimd.tensor_tensor(out=rstd[:, strips], in0=var_eps[:, strips], in1=minus_half[:], op=ALU.pow)
+            nc.gpsimd.tensor_scalar(
+                out=minus_mean[:, strips], in0=mean_var[:, strips, 0], scalar1=-1.0, scalar2=0.0,
+                op0=ALU.mult, op1=ALU.add,
+            )
+            for h in range(STRIPS):
+                b = n * STRIPS + h
+                z = keep.tile([P, CHANNELS], F32, name="z%d" % b)
+                nc.gpsimd.tensor_scalar(
+                    out=z[:], in0=x_pix[:, b, :], scalar1=minus_mean[:, b : b + 1], scalar2=rstd[:, b : b + 1],
+                    op0=ALU.add, op1=ALU.mult,
+                )
+                normed.append(z)
+
+        def image_transposes(n):
+            banks = []
+            for first_chunk in range(0, CHUNKS, 2):
+                z_t = psum_unit.tile([P, 2, IMAGE_PIXELS], F32, tag="unit", name="z_t")
+                for c in range(2):
+                    m = first_chunk + c
+                    for h in range(STRIPS):
+                        nc.tensor.transpose(
+                            out=z_t[:, c, h * P : (h + 1) * P],
+                            in_=normed[n * STRIPS + h][:, m * P : (m + 1) * P],
+                            identity=ident_f[:],
+                        )
+                banks.append(z_t)
+            return banks
+
+        def image_gain_and_shift(banks):
+            x_ln = work.tile([P, CHUNKS, IMAGE_PIXELS], BF16)
+            for m in range(CHUNKS):
+                nc.scalar.activation(
+                    out=x_ln[:, m, :],
+                    in_=banks[m // 2][:, m % 2, :],
+                    func=ACT.Identity,
+                    bias=beta[:, m : m + 1],
+                    scale=gamma[:, m : m + 1],
+                )
+            return x_ln
+
+        def image_quantise(n, x_ln):
+            x_grouped = work.tile([P, PASSES, IMAGE_PIXELS, PACK], BF16, align_bytes=64)
+            nc.vector.tensor_copy(out=x_grouped[:], in_=x_ln[:].rearrange("p (g t) s -> p g s t", t=PACK))
+            nc.vector.quantize_mx(
+                out=x_codes[:, n].rearrange("p g s -> p (g s)").bitcast(FP8X4),
+                scales=x_scales[:, n].rearrange("p g s -> p (g s)"),
+                in_=x_grouped[:].rearrange("p g s t -> p (g s t)"),
+            )
+
+        def weight_transposes(i, oc):
+            banks = []
+            for g in range(PASSES):
+                for pair in range(BANK // (2 * P)):
+                    w_t = psum_unit.tile([P, 2, 2 * P], F32, tag="unit", name="w_t")
+                    for u in range(2):
+                        for rr in range(2):
+                            r = oc * (BANK // P) + 2 * pair + rr
+                            first = 2 * P * g + u
+                            nc.tensor.transpose(
+                                out=w_t[:, u, rr * P : (rr + 1) * P],
+                                in_=w_sbs[i][:, r, :].bitcast(F32)[:, first : 2 * P * (g + 1) : 2],
+                                identity=ident_f[:],
+                            )
+                    banks.append(w_t)
+            return banks
+
+        def weight_copies(banks):
+            w_grouped = work.tile([P, PASSES * BANK * PACK], BF16, align_bytes=64)
+            w_grouped_words = w_grouped[:].bitcast(F32)
+            for k in range(UNIT_BANKS):
+                nc.scalar.copy(
+                    out=w_grouped_words[:, k * BANK : (k + 1) * BANK].rearrange("p (o u) -> p o u", u=2),
+                    in_=banks[k][:].rearrange("p u o -> p o u"),
+                )
+            return w_grouped
+
+        def weight_quantise(i, oc, w_grouped):
+            nc.vector.quantize_mx(
+                out=w_codes[i][:, oc].rearrange("p g o -> p (g o)").bitcast(FP8X4),
+                scales=w_scales[i][:, oc].rearrange("p g o -> p (g o)"),
+                in_=w_grouped[:],
+            )
+
+        def project(strip_index):
+            n, rest = divmod(strip_index, PROJECTIONS * STRIPS)
+            i, h = divmod(rest, STRIPS)
+            strip = slice(h * P, (h + 1) * P)
+            result = work.tile([P, OUTPUTS], F32, bufs=4)
+            for oc in range(HALVES):
+                acc = psum_acc.tile([P, BANK], F32)
+                for g in range(PASSES):
+                    nc.tensor.matmul_mx(
+                        out=acc[:],
+                        lhsT=x_codes[:, n, g, strip].bitcast(FP8X4),
+                        lhsT_scale=x_scales[:, n, g, strip],
+                        rhs=w_codes[i][:, oc, g, :].bitcast(FP8X4),
+                        rhs_scale=w_scales[i][:, oc, g, :],
+                        start=(g == 0),
+                        stop=(g == PASSES - 1),
+                    )
+                out_cols = slice(oc * BANK, (oc + 1) * BANK)
+                nc.vector.tensor_tensor(
+                    out=result[:, out_cols], in0=acc[:], in1=bias_sb[:, i, out_cols], op=ALU.add
+                )
+            nc.sync.dma_start(out=outs[i][n, strip, :], in_=result[:])
+
+        for n in range(IMAGES):
+            normalise_image(n)
+
+        banks = weight_transposes(0, 0)
+        w_grouped = weight_copies(banks)
+        banks = image_transposes(0)
+        weight_quantise(0, 0, w_grouped)
+
+        x_ln = image_gain_and_shift(banks)
+        banks = weight_transposes(0, 1)
+        image_quantise(0, x_ln)
+
+        projected = 0
+        weight_halves = PROJECTIONS * HALVES
+        for half_index in range(1, weight_halves):
+            i, oc = divmod(half_index, HALVES)
+            w_grouped = weight_copies(banks)
+            if half_index + 1 < weight_halves:
+                banks = weight_transposes((half_index + 1) // HALVES, (half_index + 1) % HALVES)
+            else:
+                banks = image_transposes(1)
+            weight_quantise(i, oc, w_grouped)
+            project(projected)
+            projected += 1
+
+        for n in range(1, IMAGES):
+            x_ln = image_gain_and_shift(banks)
+            if n + 1 < IMAGES:
+                banks = image_transposes(n + 1)
+            image_quantise(n, x_ln)
+            project(projected)
+            projected += 1
+
+        for strip_index in range(projected, IMAGES * PROJECTIONS * STRIPS):
+            project(strip_index)

@@ -74,8 +74,6 @@ def tile_selfscaleddotproductattention2d_pa_kernel(
             nc.sync.dma_start(out=bias_sb[:, i, :], in_=biases[i].partition_broadcast(P))
             w_sbs.append(w_sb)
 
-        ident_bf = keep.tile([P, P], BF16)
-        make_identity(nc, ident_bf[:])
         ident_f = keep.tile([P, P], F32)
         make_identity(nc, ident_f[:])
         minus_half = keep.tile([P, STRIPS], F32)
@@ -85,7 +83,7 @@ def tile_selfscaleddotproductattention2d_pa_kernel(
         nc.gpsimd.tensor_copy(out=gamma[:], in_=gamma_bf[:])
         nc.gpsimd.tensor_copy(out=beta[:], in_=beta_bf[:])
 
-        x_pix = keep.tile([P, IMAGES * STRIPS, CHANNELS], BF16)
+        x_pix = keep.tile([P, IMAGES, STRIPS * CHANNELS], BF16)
         mean_var = keep.tile([P, IMAGES * STRIPS, 2], F32)
         var_eps = keep.tile([P, IMAGES * STRIPS], F32)
         rstd = keep.tile([P, IMAGES * STRIPS], F32)
@@ -101,23 +99,22 @@ def tile_selfscaleddotproductattention2d_pa_kernel(
 
         def normalise_image(n):
             strips = slice(n * STRIPS, (n + 1) * STRIPS)
-            for h in range(STRIPS):
-                x_t = psum_unit.tile([P, CHANNELS], BF16, tag="unit", name="x_t")
-                for m in range(CHUNKS):
-                    g, t = divmod(m, PACK)
-                    first = t * IMAGE_PIXELS + h * P
+            for g in range(PASSES):
+                x_t = psum_unit.tile([P, BANK], F32, tag="unit", name="x_t")
+                for t in range(PACK):
                     nc.tensor.transpose(
-                        out=x_t[:, m * P : (m + 1) * P],
-                        in_=x_sb[:, n, g, first : first + P],
-                        identity=ident_bf[:],
+                        out=x_t[:, t * P : (t + 1) * P],
+                        in_=x_sb[:, n, g, t * IMAGE_PIXELS : (t + 1) * IMAGE_PIXELS].bitcast(F32),
+                        identity=ident_f[:],
                     )
-                nc.scalar.copy(out=x_pix[:, n * STRIPS + h, :], in_=x_t[:])
+                nc.scalar.copy(out=x_pix[:, n, :].bitcast(F32)[:, g * BANK : (g + 1) * BANK], in_=x_t[:])
             for h in range(STRIPS):
                 b = n * STRIPS + h
                 stats = work.tile([P, STATS_CALLS, STATS_DIM], F32)
                 for s in range(STATS_CALLS):
+                    first = STRIPS * s * STATS_WIDTH + h
                     nc.vector.bn_stats(
-                        out=stats[:, s, :], in_=x_pix[:, b, s * STATS_WIDTH : (s + 1) * STATS_WIDTH]
+                        out=stats[:, s, :], in_=x_pix[:, n, first : STRIPS * (s + 1) * STATS_WIDTH : STRIPS]
                     )
                 nc.vector.bn_aggr(out=mean_var[:, b, :], in_=stats[:].rearrange("p s d -> p (s d)"))
             nc.gpsimd.tensor_scalar(
@@ -133,7 +130,7 @@ def tile_selfscaleddotproductattention2d_pa_kernel(
                 b = n * STRIPS + h
                 z = keep.tile([P, CHANNELS], F32, name="z%d" % b)
                 nc.gpsimd.tensor_scalar(
-                    out=z[:], in0=x_pix[:, b, :], scalar1=minus_mean[:, b : b + 1], scalar2=rstd[:, b : b + 1],
+                    out=z[:], in0=x_pix[:, n, h :: STRIPS], scalar1=minus_mean[:, b : b + 1], scalar2=rstd[:, b : b + 1],
                     op0=ALU.add, op1=ALU.mult,
                 )
                 normed.append(z)
@@ -229,7 +226,7 @@ def tile_selfscaleddotproductattention2d_pa_kernel(
                 nc.vector.tensor_tensor(
                     out=result[:, out_cols], in0=acc[:], in1=bias_sb[:, i, out_cols], op=ALU.add
                 )
-            nc.sync.dma_start(out=outs[i][n, strip, :], in_=result[:])
+            nc.sync.dma_start(out=outs[i][n, h::STRIPS, :], in_=result[:])
 
         for n in range(IMAGES):
             normalise_image(n)

@@ -25,10 +25,12 @@ CHUNKS = CHANNELS // P
 STRIPS = IMAGE_PIXELS // P
 BANK = 512
 HALVES = OUTPUTS // BANK
-UNIT_BANKS = 4
-STATS_WIDTH = 512
-STATS_CALLS = CHANNELS // STATS_WIDTH
+ALL_HALVES = PROJECTIONS * HALVES
+HALF_ROWS = BANK // P
 STATS_DIM = 6
+
+VECTOR_SHIFT_IMAGES = 2
+STEP_PRODUCTS = 7
 
 FLOPS = 2 * IMAGES * IMAGE_PIXELS * CHANNELS * PROJECTIONS * OUTPUTS
 
@@ -43,18 +45,32 @@ def tile_selfscaleddotproductattention2d_pa_kernel(
 
     with ExitStack() as ctx:
         keep = ctx.enter_context(tc.tile_pool(name="keep", bufs=1))
-        per_weight = ctx.enter_context(tc.tile_pool(name="per_weight", bufs=PROJECTIONS))
         work = ctx.enter_context(tc.tile_pool(name="work", bufs=2))
-        psum_unit = ctx.enter_context(tc.psum_pool(name="psum_unit", bufs=UNIT_BANKS))
-        psum_acc = ctx.enter_context(tc.psum_pool(name="psum_acc", bufs=4))
+        psum = ctx.enter_context(tc.psum_pool(name="psum", bufs=8))
         ctx.enter_context(tc.manual_schedule())
 
         x_sb = keep.tile([P, IMAGES, PASSES, PACK * IMAGE_PIXELS], BF16)
-        for n in range(IMAGES):
-            nc.sync.dma_start(
-                out=x_sb[:, n], in_=x[n].rearrange("(g p t) h w -> p g (t h w)", p=P, t=PACK)
-            )
+        w_sbs = []
+        for i in range(PROJECTIONS):
+            w_sb = keep.tile([P, OUTPUTS // P, CHANNELS], BF16, name="w_sb%d" % i)
+            w_sbs.append(w_sb)
+        bias_sb = keep.tile([P, PROJECTIONS, OUTPUTS], BF16)
 
+        def load_image(n):
+            nc.sync.dma_start(out=x_sb[:, n], in_=x[n].rearrange("(g p t) h w -> p g (t h w)", p=P, t=PACK))
+
+        def load_half(k):
+            i, oc = divmod(k, HALVES)
+            rows = weights[i].rearrange("(r p) c -> p r c", p=P)
+            r_range = slice(oc * HALF_ROWS, (oc + 1) * HALF_ROWS)
+            nc.sync.dma_start(out=w_sbs[i][:, r_range, :], in_=rows[:, r_range, :])
+
+        def load_bias(i):
+            nc.sync.dma_start(out=bias_sb[:, i, :], in_=biases[i].partition_broadcast(P))
+
+        first_image = x[0].rearrange("(g p t) h w -> g p (t h w)", p=P, t=PACK)
+        for g in range(PASSES):
+            nc.sync.dma_start(out=x_sb[:, 0, g], in_=first_image[g])
         gamma_bf = keep.tile([P, CHUNKS], BF16)
         beta_bf = keep.tile([P, CHUNKS], BF16)
         for vector_sb, vector in ((gamma_bf, ln_gamma), (beta_bf, ln_beta)):
@@ -62,17 +78,16 @@ def tile_selfscaleddotproductattention2d_pa_kernel(
                 out=vector_sb[:].rearrange("p (g t) -> p g t", t=PACK),
                 in_=vector.rearrange("(g p t) -> p g t", p=P, t=PACK),
             )
-
-        w_sbs = []
-        bias_sb = keep.tile([P, PROJECTIONS, OUTPUTS], BF16)
-        for i in range(PROJECTIONS):
-            w_sb = per_weight.tile([P, OUTPUTS // P, CHANNELS], BF16, name="w_sb")
-            rows = weights[i].rearrange("(r p) k -> p r k", p=P)
+        load_image(1)
+        load_image(2)
+        load_half(0)
+        load_image(3)
+        load_half(1)
+        load_bias(0)
+        for i in range(1, PROJECTIONS):
             for oc in range(HALVES):
-                r_range = slice(oc * (BANK // P), (oc + 1) * (BANK // P))
-                nc.sync.dma_start(out=w_sb[:, r_range, :], in_=rows[:, r_range, :])
-            nc.sync.dma_start(out=bias_sb[:, i, :], in_=biases[i].partition_broadcast(P))
-            w_sbs.append(w_sb)
+                load_half(i * HALVES + oc)
+            load_bias(i)
 
         ident_f = keep.tile([P, P], F32)
         make_identity(nc, ident_f[:])
@@ -83,40 +98,40 @@ def tile_selfscaleddotproductattention2d_pa_kernel(
         nc.gpsimd.tensor_copy(out=gamma[:], in_=gamma_bf[:])
         nc.gpsimd.tensor_copy(out=beta[:], in_=beta_bf[:])
 
-        x_pix = keep.tile([P, IMAGES, STRIPS * CHANNELS], BF16)
         mean_var = keep.tile([P, IMAGES * STRIPS, 2], F32)
         var_eps = keep.tile([P, IMAGES * STRIPS], F32)
         rstd = keep.tile([P, IMAGES * STRIPS], F32)
         minus_mean = keep.tile([P, IMAGES * STRIPS], F32)
+        shift = keep.tile([P, IMAGES * STRIPS], F32)
+        normed = keep.tile([P, IMAGES * STRIPS, CHANNELS], F32)
         x_codes = keep.tile([P, IMAGES, PASSES, IMAGE_PIXELS], U32, align_bytes=64)
         x_scales = keep.tile([P, IMAGES, PASSES, IMAGE_PIXELS], U8, align_bytes=64)
-        w_codes = []
-        w_scales = []
-        for i in range(PROJECTIONS):
-            w_codes.append(per_weight.tile([P, HALVES, PASSES, BANK], U32, align_bytes=64, name="w_codes"))
-            w_scales.append(per_weight.tile([P, HALVES, PASSES, BANK], U8, align_bytes=64, name="w_scales"))
-        normed = []
+        w_codes = keep.tile([P, ALL_HALVES, PASSES, BANK], U32, align_bytes=64)
+        w_scales = keep.tile([P, ALL_HALVES, PASSES, BANK], U8, align_bytes=64)
 
-        def normalise_image(n):
-            strips = slice(n * STRIPS, (n + 1) * STRIPS)
+        def pixels_to_partitions(n):
+            banks = []
             for g in range(PASSES):
-                x_t = psum_unit.tile([P, BANK], F32, tag="unit", name="x_t")
+                x_t = psum.tile([P, BANK], F32, tag="bank", name="x_t")
                 for t in range(PACK):
                     nc.tensor.transpose(
                         out=x_t[:, t * P : (t + 1) * P],
                         in_=x_sb[:, n, g, t * IMAGE_PIXELS : (t + 1) * IMAGE_PIXELS].bitcast(F32),
                         identity=ident_f[:],
                     )
-                nc.scalar.copy(out=x_pix[:, n, :].bitcast(F32)[:, g * BANK : (g + 1) * BANK], in_=x_t[:])
+                banks.append(x_t[:].bitcast(BF16))
+            return banks
+
+        def statistics(n, banks):
+            stats = work.tile([P, STRIPS, PASSES, STATS_DIM], F32)
             for h in range(STRIPS):
-                b = n * STRIPS + h
-                stats = work.tile([P, STATS_CALLS, STATS_DIM], F32)
-                for s in range(STATS_CALLS):
-                    first = STRIPS * s * STATS_WIDTH + h
-                    nc.vector.bn_stats(
-                        out=stats[:, s, :], in_=x_pix[:, n, first : STRIPS * (s + 1) * STATS_WIDTH : STRIPS]
-                    )
-                nc.vector.bn_aggr(out=mean_var[:, b, :], in_=stats[:].rearrange("p s d -> p (s d)"))
+                for g in range(PASSES):
+                    nc.vector.bn_stats(out=stats[:, h, g, :], in_=banks[g][:, h::STRIPS])
+            for h in range(STRIPS):
+                nc.vector.bn_aggr(
+                    out=mean_var[:, n * STRIPS + h, :], in_=stats[:, h].rearrange("p g d -> p (g d)")
+                )
+            strips = slice(n * STRIPS, (n + 1) * STRIPS)
             nc.gpsimd.tensor_scalar(
                 out=var_eps[:, strips], in0=mean_var[:, strips, 1], scalar1=EPS, scalar2=1.0,
                 op0=ALU.add, op1=ALU.mult,
@@ -126,140 +141,155 @@ def tile_selfscaleddotproductattention2d_pa_kernel(
                 out=minus_mean[:, strips], in0=mean_var[:, strips, 0], scalar1=-1.0, scalar2=0.0,
                 op0=ALU.mult, op1=ALU.add,
             )
+            nc.gpsimd.tensor_tensor(
+                out=shift[:, strips], in0=minus_mean[:, strips], in1=rstd[:, strips], op=ALU.mult
+            )
+
+        def normalise(n, banks):
             for h in range(STRIPS):
                 b = n * STRIPS + h
-                z = keep.tile([P, CHANNELS], F32, name="z%d" % b)
-                nc.gpsimd.tensor_scalar(
-                    out=z[:], in0=x_pix[:, n, h :: STRIPS], scalar1=minus_mean[:, b : b + 1], scalar2=rstd[:, b : b + 1],
-                    op0=ALU.add, op1=ALU.mult,
-                )
-                normed.append(z)
+                for g in range(PASSES):
+                    nc.scalar.activation(
+                        out=normed[:, b, g * BANK : (g + 1) * BANK], in_=banks[g][:, h::STRIPS],
+                        func=ACT.Identity, bias=shift[:, b : b + 1], scale=rstd[:, b : b + 1],
+                    )
 
-        def image_transposes(n):
+        def channels_to_partitions(n):
             banks = []
             for first_chunk in range(0, CHUNKS, 2):
-                z_t = psum_unit.tile([P, 2, IMAGE_PIXELS], F32, tag="unit", name="z_t")
+                z_t = psum.tile([P, 2, IMAGE_PIXELS], F32, tag="bank", name="z_t")
                 for c in range(2):
                     m = first_chunk + c
                     for h in range(STRIPS):
                         nc.tensor.transpose(
                             out=z_t[:, c, h * P : (h + 1) * P],
-                            in_=normed[n * STRIPS + h][:, m * P : (m + 1) * P],
+                            in_=normed[:, n * STRIPS + h, m * P : (m + 1) * P],
                             identity=ident_f[:],
                         )
                 banks.append(z_t)
             return banks
 
-        def image_gain_and_shift(banks):
+        def gain_and_shift(n, banks):
             x_ln = work.tile([P, CHUNKS, IMAGE_PIXELS], BF16)
             for m in range(CHUNKS):
-                nc.scalar.activation(
-                    out=x_ln[:, m, :],
-                    in_=banks[m // 2][:, m % 2, :],
-                    func=ACT.Identity,
-                    bias=beta[:, m : m + 1],
-                    scale=gamma[:, m : m + 1],
-                )
+                source = banks[m // 2][:, m % 2, :]
+                if n < VECTOR_SHIFT_IMAGES and m >= CHUNKS // 2:
+                    nc.vector.tensor_scalar(
+                        out=x_ln[:, m, :], in0=source, scalar1=gamma[:, m : m + 1], scalar2=beta[:, m : m + 1],
+                        op0=ALU.mult, op1=ALU.add,
+                    )
+                else:
+                    nc.scalar.activation(
+                        out=x_ln[:, m, :], in_=source, func=ACT.Identity,
+                        bias=beta[:, m : m + 1], scale=gamma[:, m : m + 1],
+                    )
             return x_ln
 
-        def image_quantise(n, x_ln):
+        def group_values(x_ln):
             x_grouped = work.tile([P, PASSES, IMAGE_PIXELS, PACK], BF16, align_bytes=64)
-            nc.vector.tensor_copy(out=x_grouped[:], in_=x_ln[:].rearrange("p (g t) s -> p g s t", t=PACK))
+            for g in range(PASSES):
+                source = x_ln[:, g * PACK : (g + 1) * PACK, :].rearrange("p t s -> p s t")
+                nc.vector.tensor_copy(out=x_grouped[:, g], in_=source)
+            return x_grouped
+
+        def quantise_image(n, x_grouped):
             nc.vector.quantize_mx(
                 out=x_codes[:, n].rearrange("p g s -> p (g s)").bitcast(FP8X4),
                 scales=x_scales[:, n].rearrange("p g s -> p (g s)"),
                 in_=x_grouped[:].rearrange("p g s t -> p (g s t)"),
             )
 
-        def weight_transposes(i, oc):
+        def transpose_half(k):
+            i, oc = divmod(k, HALVES)
             banks = []
             for g in range(PASSES):
-                for pair in range(BANK // (2 * P)):
-                    w_t = psum_unit.tile([P, 2, 2 * P], F32, tag="unit", name="w_t")
+                for pair in range(HALF_ROWS // 2):
+                    w_t = psum.tile([P, 2, 2 * P], F32, tag="bank", name="w_t")
                     for u in range(2):
                         for rr in range(2):
-                            r = oc * (BANK // P) + 2 * pair + rr
-                            first = 2 * P * g + u
+                            r = oc * HALF_ROWS + 2 * pair + rr
                             nc.tensor.transpose(
                                 out=w_t[:, u, rr * P : (rr + 1) * P],
-                                in_=w_sbs[i][:, r, :].bitcast(F32)[:, first : 2 * P * (g + 1) : 2],
+                                in_=w_sbs[i][:, r, :].bitcast(F32)[:, 2 * P * g + u : 2 * P * (g + 1) : 2],
                                 identity=ident_f[:],
                             )
                     banks.append(w_t)
             return banks
 
-        def weight_copies(banks):
+        def group_words(banks):
             w_grouped = work.tile([P, PASSES * BANK * PACK], BF16, align_bytes=64)
             w_grouped_words = w_grouped[:].bitcast(F32)
-            for k in range(UNIT_BANKS):
+            for j in range(len(banks)):
                 nc.scalar.copy(
-                    out=w_grouped_words[:, k * BANK : (k + 1) * BANK].rearrange("p (o u) -> p o u", u=2),
-                    in_=banks[k][:].rearrange("p u o -> p o u"),
+                    out=w_grouped_words[:, j * BANK : (j + 1) * BANK].rearrange("p (o u) -> p o u", u=2),
+                    in_=banks[j][:].rearrange("p u o -> p o u"),
                 )
             return w_grouped
 
-        def weight_quantise(i, oc, w_grouped):
-            nc.vector.quantize_mx(
-                out=w_codes[i][:, oc].rearrange("p g o -> p (g o)").bitcast(FP8X4),
-                scales=w_scales[i][:, oc].rearrange("p g o -> p (g o)"),
-                in_=w_grouped[:],
-            )
+        def quantise_half(k, w_grouped):
+            width = BANK * PACK
+            for g in range(PASSES):
+                nc.vector.quantize_mx(
+                    out=w_codes[:, k, g, :].bitcast(FP8X4),
+                    scales=w_scales[:, k, g, :],
+                    in_=w_grouped[:, g * width : (g + 1) * width],
+                )
 
-        def project(strip_index):
-            n, rest = divmod(strip_index, PROJECTIONS * STRIPS)
-            i, h = divmod(rest, STRIPS)
-            strip = slice(h * P, (h + 1) * P)
-            result = work.tile([P, OUTPUTS], F32, bufs=4)
-            for oc in range(HALVES):
-                acc = psum_acc.tile([P, BANK], F32)
+        def product(k, n):
+            i, oc = divmod(k, HALVES)
+            out_cols = slice(oc * BANK, (oc + 1) * BANK)
+            result = work.tile([P, STRIPS, BANK], F32, bufs=6)
+            for h in range(STRIPS):
+                strip = slice(h * P, (h + 1) * P)
+                acc = psum.tile([P, BANK], F32, tag="bank", name="acc")
                 for g in range(PASSES):
                     nc.tensor.matmul_mx(
                         out=acc[:],
                         lhsT=x_codes[:, n, g, strip].bitcast(FP8X4),
                         lhsT_scale=x_scales[:, n, g, strip],
-                        rhs=w_codes[i][:, oc, g, :].bitcast(FP8X4),
-                        rhs_scale=w_scales[i][:, oc, g, :],
+                        rhs=w_codes[:, k, g, :].bitcast(FP8X4),
+                        rhs_scale=w_scales[:, k, g, :],
                         start=(g == 0),
                         stop=(g == PASSES - 1),
                     )
-                out_cols = slice(oc * BANK, (oc + 1) * BANK)
                 nc.vector.tensor_tensor(
-                    out=result[:, out_cols], in0=acc[:], in1=bias_sb[:, i, out_cols], op=ALU.add
+                    out=result[:, h, :], in0=acc[:], in1=bias_sb[:, i, out_cols], op=ALU.add
                 )
-            nc.sync.dma_start(out=outs[i][n, h::STRIPS, :], in_=result[:])
+            nc.sync.dma_start(
+                out=outs[i][n].rearrange("(p h) o -> p h o", h=STRIPS)[:, :, out_cols], in_=result[:]
+            )
 
-        for n in range(IMAGES):
-            normalise_image(n)
-
-        banks = weight_transposes(0, 0)
-        w_grouped = weight_copies(banks)
-        banks = image_transposes(0)
-        weight_quantise(0, 0, w_grouped)
-
-        x_ln = image_gain_and_shift(banks)
-        banks = weight_transposes(0, 1)
-        image_quantise(0, x_ln)
-
-        projected = 0
-        weight_halves = PROJECTIONS * HALVES
-        for half_index in range(1, weight_halves):
-            i, oc = divmod(half_index, HALVES)
-            w_grouped = weight_copies(banks)
-            if half_index + 1 < weight_halves:
-                banks = weight_transposes((half_index + 1) // HALVES, (half_index + 1) % HALVES)
-            else:
-                banks = image_transposes(1)
-            weight_quantise(i, oc, w_grouped)
-            project(projected)
-            projected += 1
-
-        for n in range(1, IMAGES):
-            x_ln = image_gain_and_shift(banks)
-            if n + 1 < IMAGES:
-                banks = image_transposes(n + 1)
-            image_quantise(n, x_ln)
-            project(projected)
-            projected += 1
-
-        for strip_index in range(projected, IMAGES * PROJECTIONS * STRIPS):
-            project(strip_index)
+        x_banks, z_banks, x_lns, x_groups = {}, {}, {}, {}
+        w_banks, w_groups = {}, {}
+        products = sorted(
+            [(k, n) for k in range(ALL_HALVES) for n in range(IMAGES)], key=lambda pair: (max(pair), pair)
+        )
+        quantised_images, quantised_halves = set(), set()
+        for step in range(-2, ALL_HALVES + 3):
+            if step + 1 in range(IMAGES):
+                statistics(step + 1, x_banks[step + 1])
+            ready = [(k, n) for k, n in products if k in quantised_halves and n in quantised_images]
+            for k, n in ready[:STEP_PRODUCTS]:
+                product(k, n)
+                products.remove((k, n))
+            if step - 1 in range(IMAGES):
+                z_banks[step - 1] = channels_to_partitions(step - 1)
+            if step - 2 in range(IMAGES):
+                quantise_image(step - 2, x_groups[step - 2])
+                quantised_images.add(step - 2)
+            if step + 2 in range(IMAGES):
+                x_banks[step + 2] = pixels_to_partitions(step + 2)
+            if step - 1 in range(IMAGES):
+                x_lns[step - 1] = gain_and_shift(step - 1, z_banks[step - 1])
+            if step in range(ALL_HALVES):
+                w_banks[step] = transpose_half(step)
+            if step in range(IMAGES):
+                normalise(step, x_banks[step])
+            if step - 1 in range(ALL_HALVES):
+                quantise_half(step - 1, w_groups[step - 1])
+                quantised_halves.add(step - 1)
+            if step - 1 in range(IMAGES):
+                x_groups[step - 1] = group_values(x_lns[step - 1])
+            if step in range(ALL_HALVES):
+                w_groups[step] = group_words(w_banks[step])
+        assert not products

@@ -30,7 +30,12 @@ HALF_ROWS = BANK // P
 STATS_DIM = 6
 
 VECTOR_SHIFT_IMAGES = 2
+LATE_STEP = IMAGES + 1
+FIRST_PRODUCTS = 1
 STEP_PRODUCTS = 7
+FIRST_SORTED_HALF = 5
+RUN = 4
+WHOLE_WEIGHTS = 1
 
 FLOPS = 2 * IMAGES * IMAGE_PIXELS * CHANNELS * PROJECTIONS * OUTPUTS
 
@@ -61,9 +66,8 @@ def tile_selfscaleddotproductattention2d_pa_kernel(
 
         def load_half(k):
             i, oc = divmod(k, HALVES)
-            rows = weights[i].rearrange("(r p) c -> p r c", p=P)
-            r_range = slice(oc * HALF_ROWS, (oc + 1) * HALF_ROWS)
-            nc.sync.dma_start(out=w_sbs[i][:, r_range, :], in_=rows[:, r_range, :])
+            rows = weights[i].rearrange("(a p r) c -> a p r c", p=P, r=HALF_ROWS)
+            nc.sync.dma_start(out=w_sbs[i][:, oc * HALF_ROWS : (oc + 1) * HALF_ROWS, :], in_=rows[oc])
 
         def load_bias(i):
             nc.sync.dma_start(out=bias_sb[:, i, :], in_=biases[i].partition_broadcast(P))
@@ -133,26 +137,35 @@ def tile_selfscaleddotproductattention2d_pa_kernel(
                 )
             strips = slice(n * STRIPS, (n + 1) * STRIPS)
             nc.gpsimd.tensor_scalar(
+                out=minus_mean[:, strips], in0=mean_var[:, strips, 0], scalar1=-1.0, scalar2=0.0,
+                op0=ALU.mult, op1=ALU.add,
+            )
+            if n == 0:
+                nc.scalar.activation(
+                    out=rstd[:, strips], in_=mean_var[:, strips, 1], func=ACT.Abs_reciprocal_sqrt, bias=EPS
+                )
+                for h in range(STRIPS):
+                    nc.scalar.activation(
+                        out=shift[:, h : h + 1], in_=minus_mean[:, h : h + 1], func=ACT.Identity,
+                        scale=rstd[:, h : h + 1],
+                    )
+                return
+            nc.gpsimd.tensor_scalar(
                 out=var_eps[:, strips], in0=mean_var[:, strips, 1], scalar1=EPS, scalar2=1.0,
                 op0=ALU.add, op1=ALU.mult,
             )
             nc.gpsimd.tensor_tensor(out=rstd[:, strips], in0=var_eps[:, strips], in1=minus_half[:], op=ALU.pow)
-            nc.gpsimd.tensor_scalar(
-                out=minus_mean[:, strips], in0=mean_var[:, strips, 0], scalar1=-1.0, scalar2=0.0,
-                op0=ALU.mult, op1=ALU.add,
-            )
             nc.gpsimd.tensor_tensor(
                 out=shift[:, strips], in0=minus_mean[:, strips], in1=rstd[:, strips], op=ALU.mult
             )
 
-        def normalise(n, banks):
-            for h in range(STRIPS):
-                b = n * STRIPS + h
-                for g in range(PASSES):
-                    nc.scalar.activation(
-                        out=normed[:, b, g * BANK : (g + 1) * BANK], in_=banks[g][:, h::STRIPS],
-                        func=ACT.Identity, bias=shift[:, b : b + 1], scale=rstd[:, b : b + 1],
-                    )
+        def normalise_strip(n, h, banks):
+            b = n * STRIPS + h
+            for g in range(PASSES):
+                nc.scalar.activation(
+                    out=normed[:, b, g * BANK : (g + 1) * BANK], in_=banks[g][:, h::STRIPS],
+                    func=ACT.Identity, bias=shift[:, b : b + 1], scale=rstd[:, b : b + 1],
+                )
 
         def channels_to_partitions(n):
             banks = []
@@ -173,7 +186,7 @@ def tile_selfscaleddotproductattention2d_pa_kernel(
             x_ln = work.tile([P, CHUNKS, IMAGE_PIXELS], BF16)
             for m in range(CHUNKS):
                 source = banks[m // 2][:, m % 2, :]
-                if n < VECTOR_SHIFT_IMAGES and m >= CHUNKS // 2:
+                if n < VECTOR_SHIFT_IMAGES and (m < CHUNKS // 2) == (n == 0):
                     nc.vector.tensor_scalar(
                         out=x_ln[:, m, :], in0=source, scalar1=gamma[:, m : m + 1], scalar2=beta[:, m : m + 1],
                         op0=ALU.mult, op1=ALU.add,
@@ -188,8 +201,10 @@ def tile_selfscaleddotproductattention2d_pa_kernel(
         def group_values(x_ln):
             x_grouped = work.tile([P, PASSES, IMAGE_PIXELS, PACK], BF16, align_bytes=64)
             for g in range(PASSES):
-                source = x_ln[:, g * PACK : (g + 1) * PACK, :].rearrange("p t s -> p s t")
-                nc.vector.tensor_copy(out=x_grouped[:, g], in_=source)
+                nc.vector.tensor_copy(
+                    out=x_grouped[:, g].rearrange("p (c i) t -> p c t i", i=RUN),
+                    in_=x_ln[:, g * PACK : (g + 1) * PACK, :].rearrange("p t (c i) -> p c t i", i=RUN),
+                )
             return x_grouped
 
         def quantise_image(n, x_grouped):
@@ -199,7 +214,17 @@ def tile_selfscaleddotproductattention2d_pa_kernel(
                 in_=x_grouped[:].rearrange("p g s t -> p (g s t)"),
             )
 
-        def transpose_half(k):
+        def sort_words(k):
+            i, oc = divmod(k, HALVES)
+            w_sorted = work.tile([P, HALF_ROWS, CHANNELS], BF16)
+            for r in range(HALF_ROWS):
+                nc.scalar.copy(
+                    out=w_sorted[:, r].bitcast(F32).rearrange("p (g u w) -> p g u w", g=PASSES, u=2),
+                    in_=w_sbs[i][:, oc * HALF_ROWS + r].bitcast(F32).rearrange("p (g w u) -> p g u w", g=PASSES, u=2),
+                )
+            return w_sorted
+
+        def transpose_half(k, w_sorted):
             i, oc = divmod(k, HALVES)
             banks = []
             for g in range(PASSES):
@@ -207,89 +232,132 @@ def tile_selfscaleddotproductattention2d_pa_kernel(
                     w_t = psum.tile([P, 2, 2 * P], F32, tag="bank", name="w_t")
                     for u in range(2):
                         for rr in range(2):
-                            r = oc * HALF_ROWS + 2 * pair + rr
+                            r = 2 * pair + rr
+                            if w_sorted is None:
+                                words = w_sbs[i][:, oc * HALF_ROWS + r, :].bitcast(F32)
+                                words = words[:, 2 * P * g + u : 2 * P * (g + 1) : 2]
+                            else:
+                                words = w_sorted[:, r, :].bitcast(F32)
+                                words = words[:, P * (2 * g + u) : P * (2 * g + u + 1)]
                             nc.tensor.transpose(
-                                out=w_t[:, u, rr * P : (rr + 1) * P],
-                                in_=w_sbs[i][:, r, :].bitcast(F32)[:, 2 * P * g + u : 2 * P * (g + 1) : 2],
-                                identity=ident_f[:],
+                                out=w_t[:, u, rr * P : (rr + 1) * P], in_=words, identity=ident_f[:]
                             )
                     banks.append(w_t)
             return banks
 
         def group_words(banks):
             w_grouped = work.tile([P, PASSES * BANK * PACK], BF16, align_bytes=64)
-            w_grouped_words = w_grouped[:].bitcast(F32)
-            for j in range(len(banks)):
-                nc.scalar.copy(
-                    out=w_grouped_words[:, j * BANK : (j + 1) * BANK].rearrange("p (o u) -> p o u", u=2),
-                    in_=banks[j][:].rearrange("p u o -> p o u"),
-                )
+            words = w_grouped[:].bitcast(F32).rearrange(
+                "p (g o pair rr u) -> p g pair o rr u", g=PASSES, pair=HALF_ROWS // 2, rr=2, u=2
+            )
+            for g in range(PASSES):
+                for pair in range(HALF_ROWS // 2):
+                    nc.scalar.copy(
+                        out=words[:, g, pair],
+                        in_=banks[g * (HALF_ROWS // 2) + pair][:].rearrange("p u (rr o) -> p o rr u", rr=2),
+                    )
             return w_grouped
 
         def quantise_half(k, w_grouped):
-            width = BANK * PACK
-            for g in range(PASSES):
-                nc.vector.quantize_mx(
-                    out=w_codes[:, k, g, :].bitcast(FP8X4),
-                    scales=w_scales[:, k, g, :],
-                    in_=w_grouped[:, g * width : (g + 1) * width],
-                )
-
-        def product(k, n):
-            i, oc = divmod(k, HALVES)
-            out_cols = slice(oc * BANK, (oc + 1) * BANK)
-            result = work.tile([P, STRIPS, BANK], F32, bufs=6)
-            for h in range(STRIPS):
-                strip = slice(h * P, (h + 1) * P)
-                acc = psum.tile([P, BANK], F32, tag="bank", name="acc")
-                for g in range(PASSES):
-                    nc.tensor.matmul_mx(
-                        out=acc[:],
-                        lhsT=x_codes[:, n, g, strip].bitcast(FP8X4),
-                        lhsT_scale=x_scales[:, n, g, strip],
-                        rhs=w_codes[:, k, g, :].bitcast(FP8X4),
-                        rhs_scale=w_scales[:, k, g, :],
-                        start=(g == 0),
-                        stop=(g == PASSES - 1),
-                    )
-                nc.vector.tensor_tensor(
-                    out=result[:, h, :], in0=acc[:], in1=bias_sb[:, i, out_cols], op=ALU.add
-                )
-            nc.sync.dma_start(
-                out=outs[i][n].rearrange("(p h) o -> p h o", h=STRIPS)[:, :, out_cols], in_=result[:]
+            nc.vector.quantize_mx(
+                out=w_codes[:, k].rearrange("p g o -> p (g o)").bitcast(FP8X4),
+                scales=w_scales[:, k].rearrange("p g o -> p (g o)"),
+                in_=w_grouped[:],
             )
 
+        def one_bank(k, n, h, result):
+            i, oc = divmod(k, HALVES)
+            strip = slice(h * P, (h + 1) * P)
+            acc = psum.tile([P, BANK], F32, tag="bank", name="acc")
+            for g in range(PASSES):
+                nc.tensor.matmul_mx(
+                    out=acc[:],
+                    lhsT=x_codes[:, n, g, strip].bitcast(FP8X4),
+                    lhsT_scale=x_scales[:, n, g, strip],
+                    rhs=w_codes[:, k, g, :].bitcast(FP8X4),
+                    rhs_scale=w_scales[:, k, g, :],
+                    start=(g == 0),
+                    stop=(g == PASSES - 1),
+                )
+            nc.vector.tensor_tensor(
+                out=result, in0=acc[:], in1=bias_sb[:, i, oc * BANK : (oc + 1) * BANK], op=ALU.add
+            )
+
+        def product(halves, n):
+            i, oc = divmod(halves[0], HALVES)
+            out_strips = outs[i][n].rearrange("(p h) o -> p h o", h=STRIPS)
+            if len(halves) == HALVES:
+                for h in range(STRIPS):
+                    result = work.tile([P, OUTPUTS], F32, bufs=6, name="result")
+                    for k in halves:
+                        one_bank(k, n, h, result[:, (k % HALVES) * BANK : (k % HALVES + 1) * BANK])
+                    nc.sync.dma_start(out=out_strips[:, h, :], in_=result[:])
+            else:
+                result = work.tile([P, STRIPS * BANK], F32, bufs=6, name="result")
+                for h in range(STRIPS):
+                    one_bank(halves[0], n, h, result[:, h * BANK : (h + 1) * BANK])
+                nc.sync.dma_start(
+                    out=out_strips[:, :, oc * BANK : (oc + 1) * BANK],
+                    in_=result[:].rearrange("p (h o) -> p h o", h=STRIPS),
+                )
+
         x_banks, z_banks, x_lns, x_groups = {}, {}, {}, {}
-        w_banks, w_groups = {}, {}
-        products = sorted(
-            [(k, n) for k in range(ALL_HALVES) for n in range(IMAGES)], key=lambda pair: (max(pair), pair)
-        )
+        w_banks, w_groups, sorted_words = {}, {}, {}
+        products = []
+        for n in range(IMAGES):
+            whole = WHOLE_WEIGHTS if n > 0 else 0
+            products += [(tuple(range(i * HALVES, (i + 1) * HALVES)), n) for i in range(whole)]
+            products += [((k,), n) for k in range(whole * HALVES, ALL_HALVES)]
+        products.sort(key=lambda pair: (max(pair[0][-1], pair[1]), pair))
         quantised_images, quantised_halves = set(), set()
+
+        def multiply(room):
+            for halves, n in list(products):
+                ready = n in quantised_images and all(k in quantised_halves for k in halves)
+                if ready and len(halves) <= room:
+                    product(halves, n)
+                    products.remove((halves, n))
+                    room -= len(halves)
+            return room
+
+        def next_image(n):
+            if n in range(IMAGES) and n not in quantised_images:
+                quantise_image(n, x_groups[n])
+                quantised_images.add(n)
+
+        def next_half(k):
+            if k in range(ALL_HALVES) and k not in quantised_halves:
+                quantise_half(k, w_groups[k])
+                quantised_halves.add(k)
+
         for step in range(-2, ALL_HALVES + 3):
+            if step == 2:
+                next_image(0)
             if step + 1 in range(IMAGES):
                 statistics(step + 1, x_banks[step + 1])
-            ready = [(k, n) for k, n in products if k in quantised_halves and n in quantised_images]
-            for k, n in ready[:STEP_PRODUCTS]:
-                product(k, n)
-                products.remove((k, n))
+            room = STEP_PRODUCTS
+            if step >= LATE_STEP:
+                room += multiply(FIRST_PRODUCTS) - FIRST_PRODUCTS
+                next_image(step - 2)
+                next_half(step - 1)
+            multiply(room)
             if step - 1 in range(IMAGES):
                 z_banks[step - 1] = channels_to_partitions(step - 1)
-            if step - 2 in range(IMAGES):
-                quantise_image(step - 2, x_groups[step - 2])
-                quantised_images.add(step - 2)
+            next_image(step - 2)
             if step + 2 in range(IMAGES):
                 x_banks[step + 2] = pixels_to_partitions(step + 2)
             if step - 1 in range(IMAGES):
                 x_lns[step - 1] = gain_and_shift(step - 1, z_banks[step - 1])
             if step in range(ALL_HALVES):
-                w_banks[step] = transpose_half(step)
+                w_banks[step] = transpose_half(step, sorted_words.get(step))
             if step in range(IMAGES):
-                normalise(step, x_banks[step])
-            if step - 1 in range(ALL_HALVES):
-                quantise_half(step - 1, w_groups[step - 1])
-                quantised_halves.add(step - 1)
+                for h in range(STRIPS):
+                    normalise_strip(step, h, x_banks[step])
+            next_half(step - 1)
             if step - 1 in range(IMAGES):
                 x_groups[step - 1] = group_values(x_lns[step - 1])
             if step in range(ALL_HALVES):
                 w_groups[step] = group_words(w_banks[step])
+            if step + 1 in range(FIRST_SORTED_HALF, ALL_HALVES):
+                sorted_words[step + 1] = sort_words(step + 1)
         assert not products

from contextlib import ExitStack

import concourse.mybir as mybir
from concourse.masks import make_identity

BF16 = mybir.dt.bfloat16
F32 = mybir.dt.float32
U32 = mybir.dt.uint32
U8 = mybir.dt.uint8
FP8X4 = mybir.dt.float8_e4m3fn_x4
ACT = mybir.ActivationFunctionType
ALU = mybir.AluOpType

P = 128
IMAGES = 4
CHANNELS = 1024
IMAGE_PIXELS = 256
OUTPUTS = 1024
PROJECTIONS = 3
EPS = 1e-5

PACK = 4
PASSES = CHANNELS // (P * PACK)
CHUNKS = CHANNELS // P
STRIPS = IMAGE_PIXELS // P
BANK = 512
HALVES = OUTPUTS // BANK
ALL_HALVES = PROJECTIONS * HALVES
HALF_ROWS = BANK // P
STATS_DIM = 6

VECTOR_SHIFT_IMAGES = 2
LATE_STEP = IMAGES + 1
FIRST_PRODUCTS = 1
STEP_PRODUCTS = 7
FIRST_SORTED_HALF = 5
RUN = 4
WHOLE_WEIGHTS = 1

FLOPS = 2 * IMAGES * IMAGE_PIXELS * CHANNELS * PROJECTIONS * OUTPUTS


def tile_selfscaleddotproductattention2d_pa_kernel(
    tc, x, ln_gamma, ln_beta, Wq, bq, Wk, bk, Wv, bv, out_0, out_1, out_2
):
    nc = tc.nc
    weights = (Wq, Wk, Wv)
    biases = (bq, bk, bv)
    outs = (out_0, out_1, out_2)

    with ExitStack() as ctx:
        keep = ctx.enter_context(tc.tile_pool(name="keep", bufs=1))
        work = ctx.enter_context(tc.tile_pool(name="work", bufs=2))
        psum = ctx.enter_context(tc.psum_pool(name="psum", bufs=8))
        ctx.enter_context(tc.manual_schedule())

        x_sb = keep.tile([P, IMAGES, PASSES, PACK * IMAGE_PIXELS], BF16)
        w_sbs = []
        for i in range(PROJECTIONS):
            w_sb = keep.tile([P, OUTPUTS // P, CHANNELS], BF16, name="w_sb%d" % i)
            w_sbs.append(w_sb)
        bias_sb = keep.tile([P, PROJECTIONS, OUTPUTS], BF16)

        def load_image(n):
            nc.sync.dma_start(out=x_sb[:, n], in_=x[n].rearrange("(g p t) h w -> p g (t h w)", p=P, t=PACK))

        def load_half(k):
            i, oc = divmod(k, HALVES)
            rows = weights[i].rearrange("(a p r) c -> a p r c", p=P, r=HALF_ROWS)
            nc.sync.dma_start(out=w_sbs[i][:, oc * HALF_ROWS : (oc + 1) * HALF_ROWS, :], in_=rows[oc])

        def load_bias(i):
            nc.sync.dma_start(out=bias_sb[:, i, :], in_=biases[i].partition_broadcast(P))

        first_image = x[0].rearrange("(g p t) h w -> g p (t h w)", p=P, t=PACK)
        for g in range(PASSES):
            nc.sync.dma_start(out=x_sb[:, 0, g], in_=first_image[g])
        gamma_bf = keep.tile([P, CHUNKS], BF16)
        beta_bf = keep.tile([P, CHUNKS], BF16)
        for vector_sb, vector in ((gamma_bf, ln_gamma), (beta_bf, ln_beta)):
            nc.scalar.dma_start(
                out=vector_sb[:].rearrange("p (g t) -> p g t", t=PACK),
                in_=vector.rearrange("(g p t) -> p g t", p=P, t=PACK),
            )
        load_image(1)
        load_image(2)
        load_half(0)
        load_image(3)
        load_half(1)
        load_bias(0)
        for i in range(1, PROJECTIONS):
            for oc in range(HALVES):
                load_half(i * HALVES + oc)
            load_bias(i)

        ident_f = keep.tile([P, P], F32)
        make_identity(nc, ident_f[:])
        minus_half = keep.tile([P, STRIPS], F32)
        nc.gpsimd.memset(minus_half[:], -0.5)
        gamma = keep.tile([P, CHUNKS], F32)
        beta = keep.tile([P, CHUNKS], F32)
        nc.gpsimd.tensor_copy(out=gamma[:], in_=gamma_bf[:])
        nc.gpsimd.tensor_copy(out=beta[:], in_=beta_bf[:])

        mean_var = keep.tile([P, IMAGES * STRIPS, 2], F32)
        var_eps = keep.tile([P, IMAGES * STRIPS], F32)
        rstd = keep.tile([P, IMAGES * STRIPS], F32)
        minus_mean = keep.tile([P, IMAGES * STRIPS], F32)
        shift = keep.tile([P, IMAGES * STRIPS], F32)
        normed = keep.tile([P, IMAGES * STRIPS, CHANNELS], F32)
        x_codes = keep.tile([P, IMAGES, PASSES, IMAGE_PIXELS], U32, align_bytes=64)
        x_scales = keep.tile([P, IMAGES, PASSES, IMAGE_PIXELS], U8, align_bytes=64)
        w_codes = keep.tile([P, ALL_HALVES, PASSES, BANK], U32, align_bytes=64)
        w_scales = keep.tile([P, ALL_HALVES, PASSES, BANK], U8, align_bytes=64)

        def pixels_to_partitions(n):
            banks = []
            for g in range(PASSES):
                x_t = psum.tile([P, BANK], F32, tag="bank", name="x_t")
                for t in range(PACK):
                    nc.tensor.transpose(
                        out=x_t[:, t * P : (t + 1) * P],
                        in_=x_sb[:, n, g, t * IMAGE_PIXELS : (t + 1) * IMAGE_PIXELS].bitcast(F32),
                        identity=ident_f[:],
                    )
                banks.append(x_t[:].bitcast(BF16))
            return banks

        def statistics(n, banks):
            stats = work.tile([P, STRIPS, PASSES, STATS_DIM], F32)
            for h in range(STRIPS):
                for g in range(PASSES):
                    nc.vector.bn_stats(out=stats[:, h, g, :], in_=banks[g][:, h::STRIPS])
            for h in range(STRIPS):
                nc.vector.bn_aggr(
                    out=mean_var[:, n * STRIPS + h, :], in_=stats[:, h].rearrange("p g d -> p (g d)")
                )
            strips = slice(n * STRIPS, (n + 1) * STRIPS)
            nc.gpsimd.tensor_scalar(
                out=minus_mean[:, strips], in0=mean_var[:, strips, 0], scalar1=-1.0, scalar2=0.0,
                op0=ALU.mult, op1=ALU.add,
            )
            if n == 0:
                nc.scalar.activation(
                    out=rstd[:, strips], in_=mean_var[:, strips, 1], func=ACT.Abs_reciprocal_sqrt, bias=EPS
                )
                for h in range(STRIPS):
                    nc.scalar.activation(
                        out=shift[:, h : h + 1], in_=minus_mean[:, h : h + 1], func=ACT.Identity,
                        scale=rstd[:, h : h + 1],
                    )
                return
            nc.gpsimd.tensor_scalar(
                out=var_eps[:, strips], in0=mean_var[:, strips, 1], scalar1=EPS, scalar2=1.0,
                op0=ALU.add, op1=ALU.mult,
            )
            nc.gpsimd.tensor_tensor(out=rstd[:, strips], in0=var_eps[:, strips], in1=minus_half[:], op=ALU.pow)
            nc.gpsimd.tensor_tensor(
                out=shift[:, strips], in0=minus_mean[:, strips], in1=rstd[:, strips], op=ALU.mult
            )

        def normalise_strip(n, h, banks):
            b = n * STRIPS + h
            for g in range(PASSES):
                nc.scalar.activation(
                    out=normed[:, b, g * BANK : (g + 1) * BANK], in_=banks[g][:, h::STRIPS],
                    func=ACT.Identity, bias=shift[:, b : b + 1], scale=rstd[:, b : b + 1],
                )

        def channels_to_partitions(n):
            banks = []
            for first_chunk in range(0, CHUNKS, 2):
                z_t = psum.tile([P, 2, IMAGE_PIXELS], F32, tag="bank", name="z_t")
                for c in range(2):
                    m = first_chunk + c
                    for h in range(STRIPS):
                        nc.tensor.transpose(
                            out=z_t[:, c, h * P : (h + 1) * P],
                            in_=normed[:, n * STRIPS + h, m * P : (m + 1) * P],
                            identity=ident_f[:],
                        )
                banks.append(z_t)
            return banks

        def gain_and_shift(n, banks):
            x_ln = work.tile([P, CHUNKS, IMAGE_PIXELS], BF16)
            for m in range(CHUNKS):
                source = banks[m // 2][:, m % 2, :]
                if n < VECTOR_SHIFT_IMAGES and (m < CHUNKS // 2) == (n == 0):
                    nc.vector.tensor_scalar(
                        out=x_ln[:, m, :], in0=source, scalar1=gamma[:, m : m + 1], scalar2=beta[:, m : m + 1],
                        op0=ALU.mult, op1=ALU.add,
                    )
                else:
                    nc.scalar.activation(
                        out=x_ln[:, m, :], in_=source, func=ACT.Identity,
                        bias=beta[:, m : m + 1], scale=gamma[:, m : m + 1],
                    )
            return x_ln

        def group_values(x_ln):
            x_grouped = work.tile([P, PASSES, IMAGE_PIXELS, PACK], BF16, align_bytes=64)
            for g in range(PASSES):
                nc.vector.tensor_copy(
                    out=x_grouped[:, g].rearrange("p (c i) t -> p c t i", i=RUN),
                    in_=x_ln[:, g * PACK : (g + 1) * PACK, :].rearrange("p t (c i) -> p c t i", i=RUN),
                )
            return x_grouped

        def quantise_image(n, x_grouped):
            nc.vector.quantize_mx(
                out=x_codes[:, n].rearrange("p g s -> p (g s)").bitcast(FP8X4),
                scales=x_scales[:, n].rearrange("p g s -> p (g s)"),
                in_=x_grouped[:].rearrange("p g s t -> p (g s t)"),
            )

        def sort_words(k):
            i, oc = divmod(k, HALVES)
            w_sorted = work.tile([P, HALF_ROWS, CHANNELS], BF16)
            for r in range(HALF_ROWS):
                nc.scalar.copy(
                    out=w_sorted[:, r].bitcast(F32).rearrange("p (g u w) -> p g u w", g=PASSES, u=2),
                    in_=w_sbs[i][:, oc * HALF_ROWS + r].bitcast(F32).rearrange("p (g w u) -> p g u w", g=PASSES, u=2),
                )
            return w_sorted

        def transpose_half(k, w_sorted):
            i, oc = divmod(k, HALVES)
            banks = []
            for g in range(PASSES):
                for pair in range(HALF_ROWS // 2):
                    w_t = psum.tile([P, 2, 2 * P], F32, tag="bank", name="w_t")
                    for u in range(2):
                        for rr in range(2):
                            r = 2 * pair + rr
                            if w_sorted is None:
                                words = w_sbs[i][:, oc * HALF_ROWS + r, :].bitcast(F32)
                                words = words[:, 2 * P * g + u : 2 * P * (g + 1) : 2]
                            else:
                                words = w_sorted[:, r, :].bitcast(F32)
                                words = words[:, P * (2 * g + u) : P * (2 * g + u + 1)]
                            nc.tensor.transpose(
                                out=w_t[:, u, rr * P : (rr + 1) * P], in_=words, identity=ident_f[:]
                            )
                    banks.append(w_t)
            return banks

        def group_words(banks):
            w_grouped = work.tile([P, PASSES * BANK * PACK], BF16, align_bytes=64)
            words = w_grouped[:].bitcast(F32).rearrange(
                "p (g o pair rr u) -> p g pair o rr u", g=PASSES, pair=HALF_ROWS // 2, rr=2, u=2
            )
            for g in range(PASSES):
                for pair in range(HALF_ROWS // 2):
                    nc.scalar.copy(
                        out=words[:, g, pair],
                        in_=banks[g * (HALF_ROWS // 2) + pair][:].rearrange("p u (rr o) -> p o rr u", rr=2),
                    )
            return w_grouped

        def quantise_half(k, w_grouped):
            nc.vector.quantize_mx(
                out=w_codes[:, k].rearrange("p g o -> p (g o)").bitcast(FP8X4),
                scales=w_scales[:, k].rearrange("p g o -> p (g o)"),
                in_=w_grouped[:],
            )

        def one_bank(k, n, h, result):
            i, oc = divmod(k, HALVES)
            strip = slice(h * P, (h + 1) * P)
            acc = psum.tile([P, BANK], F32, tag="bank", name="acc")
            for g in range(PASSES):
                nc.tensor.matmul_mx(
                    out=acc[:],
                    lhsT=x_codes[:, n, g, strip].bitcast(FP8X4),
                    lhsT_scale=x_scales[:, n, g, strip],
                    rhs=w_codes[:, k, g, :].bitcast(FP8X4),
                    rhs_scale=w_scales[:, k, g, :],
                    start=(g == 0),
                    stop=(g == PASSES - 1),
                )
            nc.vector.tensor_tensor(
                out=result, in0=acc[:], in1=bias_sb[:, i, oc * BANK : (oc + 1) * BANK], op=ALU.add
            )

        def product(halves, n):
            i, oc = divmod(halves[0], HALVES)
            out_strips = outs[i][n].rearrange("(p h) o -> p h o", h=STRIPS)
            if len(halves) == HALVES:
                for h in range(STRIPS):
                    result = work.tile([P, OUTPUTS], F32, bufs=6, name="result")
                    for k in halves:
                        one_bank(k, n, h, result[:, (k % HALVES) * BANK : (k % HALVES + 1) * BANK])
                    nc.sync.dma_start(out=out_strips[:, h, :], in_=result[:])
            else:
                result = work.tile([P, STRIPS * BANK], F32, bufs=6, name="result")
                for h in range(STRIPS):
                    one_bank(halves[0], n, h, result[:, h * BANK : (h + 1) * BANK])
                nc.sync.dma_start(
                    out=out_strips[:, :, oc * BANK : (oc + 1) * BANK],
                    in_=result[:].rearrange("p (h o) -> p h o", h=STRIPS),
                )

        x_banks, z_banks, x_lns, x_groups = {}, {}, {}, {}
        w_banks, w_groups, sorted_words = {}, {}, {}
        products = []
        for n in range(IMAGES):
            whole = WHOLE_WEIGHTS if n > 0 else 0
            products += [(tuple(range(i * HALVES, (i + 1) * HALVES)), n) for i in range(whole)]
            products += [((k,), n) for k in range(whole * HALVES, ALL_HALVES)]
        products.sort(key=lambda pair: (max(pair[0][-1], pair[1]), pair))
        quantised_images, quantised_halves = set(), set()

        def multiply(room):
            for halves, n in list(products):
                ready = n in quantised_images and all(k in quantised_halves for k in halves)
                if ready and len(halves) <= room:
                    product(halves, n)
                    products.remove((halves, n))
                    room -= len(halves)
            return room

        def next_image(n):
            if n in range(IMAGES) and n not in quantised_images:
                quantise_image(n, x_groups[n])
                quantised_images.add(n)

        def next_half(k):
            if k in range(ALL_HALVES) and k not in quantised_halves:
                quantise_half(k, w_groups[k])
                quantised_halves.add(k)

        for step in range(-2, ALL_HALVES + 3):
            if step == 2:
                next_image(0)
            if step + 1 in range(IMAGES):
                statistics(step + 1, x_banks[step + 1])
            room = STEP_PRODUCTS
            if step >= LATE_STEP:
                room += multiply(FIRST_PRODUCTS) - FIRST_PRODUCTS
                next_image(step - 2)
                next_half(step - 1)
            multiply(room)
            if step - 1 in range(IMAGES):
                z_banks[step - 1] = channels_to_partitions(step - 1)
            next_image(step - 2)
            if step + 2 in range(IMAGES):
                x_banks[step + 2] = pixels_to_partitions(step + 2)
            if step - 1 in range(IMAGES):
                x_lns[step - 1] = gain_and_shift(step - 1, z_banks[step - 1])
            if step in range(ALL_HALVES):
                w_banks[step] = transpose_half(step, sorted_words.get(step))
            if step in range(IMAGES):
                for h in range(STRIPS):
                    normalise_strip(step, h, x_banks[step])
            next_half(step - 1)
            if step - 1 in range(IMAGES):
                x_groups[step - 1] = group_values(x_lns[step - 1])
            if step in range(ALL_HALVES):
                w_groups[step] = group_words(w_banks[step])
            if step + 1 in range(FIRST_SORTED_HALF, ALL_HALVES):
                sorted_words[step + 1] = sort_words(step + 1)
        assert not products
